import numpy as np
import ml_dtypes


def mxq(x, axis, fmt="e4m3"):
    dtype, down = {"e4m3": (ml_dtypes.float8_e4m3fn, 7), "e5m2": (ml_dtypes.float8_e5m2, 14)}[fmt]
    v = np.moveaxis(np.asarray(x, np.float32).astype(ml_dtypes.bfloat16).astype(np.float64), axis, -1)
    blocks = v.reshape(v.shape[:-1] + (-1, 32))
    amax = np.abs(blocks).max(-1, keepdims=True)
    byte = np.maximum(np.where(amax > 0, np.frexp(amax)[1] - 1 + 127, 0) - down, 1)
    scale = np.exp2(byte - 127.0)
    codes = (blocks / scale).astype(np.float32).astype(dtype).astype(np.float64)
    return np.moveaxis((codes * scale).reshape(v.shape), -1, axis)


WIDE = False


def mx_kscale(k):
    if not WIDE:
        return np.ones(k)
    levels = np.array([30, -30])
    if k % 512:
        return np.exp2(np.random.permutation(np.resize(levels, k // 32))).repeat(32)
    a = np.empty((k // 512, 16))
    for p in range(k // 512):
        a[p, :8] = np.random.permutation(np.resize(levels, 8))
        for g in range(8):
            far = levels[np.abs(levels - a[p, g]) >= 10]
            a[p, g + 8] = far[np.random.randint(len(far))]
    return np.exp2(a.ravel()).repeat(32)


BF16 = ml_dtypes.bfloat16


def bf(x):
    return np.asarray(x, np.float32).astype(BF16)


def f64(x):
    return np.asarray(x).astype(np.float64)


B, S, D, H, DK = 4, 128, 2048, 16, 128
E = H * DK
HALF = DK // 2


def rope(t, cos2, sin2):
    t_even = t[..., 0::2]
    t_odd = t[..., 1::2]
    rot = np.stack([-t_odd, t_even], axis=-1).reshape(t.shape)
    return t * cos2 + rot * sin2


def setup_inputs():
    s = mx_kscale(D)
    ang = np.random.uniform(-np.pi, np.pi, (S, HALF))
    return {"x": bf(np.random.standard_normal((B, S, D)) * s),
            "Wq": bf(np.random.standard_normal((D, E)) / np.sqrt(D) / s[:, None]),
            "Wk": bf(np.random.standard_normal((D, E)) / np.sqrt(D) / s[:, None]),
            "cos2": bf(np.repeat(np.cos(ang), 2, axis=-1)),
            "sin2": bf(np.repeat(np.sin(ang), 2, axis=-1))}


def reference(x, Wq, Wk, cos2, sin2):
    xq = mxq(f64(x), 2, "e5m2")
    q = (xq @ mxq(f64(Wq), 0, "e5m2")).reshape(B, S, H, DK).swapaxes(1, 2)
    k = (xq @ mxq(f64(Wk), 0, "e5m2")).reshape(B, S, H, DK).swapaxes(1, 2)
    c, sn = f64(cos2), f64(sin2)
    return rope(q, c, sn), rope(k, c, sn)

@@ -1,0 +1,246 @@
+from contextlib import ExitStack
+
+import concourse.mybir as mybir
+from concourse.masks import make_identity
+
+F32 = mybir.dt.float32
+BF16 = mybir.dt.bfloat16
+U32 = mybir.dt.uint32
+U8 = mybir.dt.uint8
+FP8X4 = mybir.dt.float8_e5m2_x4
+ALU = mybir.AluOpType
+
+B, S, D, H, DK = 4, 128, 2048, 16, 128
+E = H * DK
+P = 128
+PACK = 4
+K_PASS = P * PACK
+PASSES = D // K_PASS
+N = 512
+HEADS = N // DK
+CHUNKS_PER_W = E // N
+CHUNKS = 2 * CHUNKS_PER_W
+AHEAD = 3
+HEAD_V_COLS = 320
+V_COLS = 256
+V_ADD = 128
+ACC_BANKS = 5
+COS_AT = 1
+
+FLOPS = 2 * 2 * B * S * D * E
+
+
+def tile_multiheadselfattention_pa_kernel(tc, x, Wq, Wk, cos2, sin2, out_0, out_1):
+    nc = tc.nc
+    weights = (Wq, Wk)
+    outs = (out_0, out_1)
+
+    with ExitStack() as ctx:
+        keep = ctx.enter_context(tc.tile_pool(name="keep", bufs=1))
+        ring = ctx.enter_context(tc.tile_pool(name="ring", bufs=2))
+        psum = ctx.enter_context(tc.psum_pool(name="psum", bufs=1))
+        ctx.enter_context(tc.manual_schedule())
+
+        ident = keep.tile([P, P], F32, name="ident")
+        cos_sb = keep.tile([P, DK], BF16, name="cos_sb")
+        sin_sb = keep.tile([P, DK], BF16, name="sin_sb")
+        sin_signed = keep.tile([P, DK], F32, name="sin_signed")
+        x_codes = keep.tile([P, B, PASSES * S], U32, name="x_codes", align_bytes=64)
+        x_scales = keep.tile([P, B, PASSES * S], U8, name="x_scales", align_bytes=64)
+
+        x_raw, x_grouped, w_raw, w_grouped, w_codes, w_scales = {}, {}, {}, {}, {}, {}
+        x_banks, acc, by_cos, by_sin, rotated = {}, {}, {}, {}, {}
+
+        def bank(i):
+            return psum.tile([P, N], F32, name="bank%d" % i)
+
+        def load_x(b):
+            x_raw[b] = keep.tile([P, D], BF16, name="x_raw%d" % b)
+            nc.sync.dma_start(out=x_raw[b][:], in_=x[b])
+
+        def load_w(c, g):
+            w = weights[c // CHUNKS_PER_W]
+            n0 = (c % CHUNKS_PER_W) * N
+            w_raw[c, g] = ring.tile([P, PACK, N], BF16, name="w_raw", bufs=(AHEAD + 1) * PASSES)
+            rows = w[g * K_PASS : (g + 1) * K_PASS, n0 : n0 + N]
+            nc.sync.dma_start(out=w_raw[c, g][:], in_=rows.rearrange("(p t) n -> p t n", t=PACK))
+
+        def transpose_x(b):
+            words = x_raw[b][:].bitcast(F32)
+            for half in range(2):
+                xt = bank(4 + 2 * (b % 2) + half)
+                x_banks[b, half] = xt
+                for gg in range(2):
+                    g = 2 * half + gg
+                    for u in range(2):
+                        col = (2 * gg + u) * S
+                        nc.tensor.transpose(
+                            xt[:, col : col + S], words[:, 256 * g + u : 256 * (g + 1) : 2], ident[:]
+                        )
+
+        def copy_x(b):
+            x_grouped[b] = ring.tile([P, D], BF16, name="x_grouped", bufs=2, align_bytes=64)
+            words = x_grouped[b][:].bitcast(F32)
+            for half in range(2):
+                nc.scalar.copy(
+                    out=words[:, half * N : (half + 1) * N].rearrange("p (g s u) -> p g s u", g=2, u=2),
+                    in_=x_banks[b, half][:].rearrange("p (g u s) -> p g s u", g=2, u=2),
+                )
+
+        def quantize_x(b):
+            nc.vector.quantize_mx(
+                out=x_codes[:, b, :].bitcast(FP8X4), scales=x_scales[:, b, :], in_=x_grouped[b][:]
+            )
+
+        def last_before_rotation(c):
+            return (c + 1, 1)
+
+        def shared_tag(c):
+            return "shared%d" % (c % 3)
+
+        def interleave(engine, c, g, n0, n1):
+            if n0 == n1:
+                return
+            if (c, g) not in w_grouped:
+                holders = [cc for cc in range(1, CHUNKS) if last_before_rotation(cc) == (c, g)]
+                if holders:
+                    w_grouped[c, g] = ring.tile([P, N, PACK], BF16, name=shared_tag(holders[0]), bufs=1, align_bytes=64)
+                else:
+                    w_grouped[c, g] = ring.tile([P, N, PACK], BF16, name="w_grouped", bufs=7, align_bytes=64)
+            dst = w_grouped[c, g][:, n0:n1, :].rearrange("p (n i) t -> p n t i", i=4)
+            src = w_raw[c, g][:, :, n0:n1].rearrange("p t (n i) -> p n t i", i=4)
+            if engine == "vector":
+                nc.vector.tensor_copy(out=dst, in_=src)
+            else:
+                nc.scalar.copy(out=dst, in_=src)
+
+        def quantize_w(c, g):
+            w_codes[c, g] = ring.tile([P, N], U32, name="w_codes", bufs=8, align_bytes=64)
+            w_scales[c, g] = ring.tile([P, N], U8, name="w_scales", bufs=8, align_bytes=64)
+            nc.vector.quantize_mx(
+                out=w_codes[c, g][:].bitcast(FP8X4),
+                scales=w_scales[c, g][:],
+                in_=w_grouped[c, g][:].rearrange("p n t -> p (n t)"),
+            )
+
+        def multiply(c, g, b):
+            if g == 0:
+                acc[c, b] = bank((B * c + b) % ACC_BANKS)
+            cols = slice(g * S, (g + 1) * S)
+            nc.tensor.matmul_mx(
+                out=acc[c, b][:],
+                lhsT=x_codes[:, b, cols].bitcast(FP8X4),
+                lhsT_scale=x_scales[:, b, cols],
+                rhs=w_codes[c, g][:].bitcast(FP8X4),
+                rhs_scale=w_scales[c, g][:],
+                start=(g == 0),
+                stop=(g == PASSES - 1),
+            )
+
+        def products(c, b):
+            if b == 0:
+                by_cos[c] = ring.tile([P, B * N], F32, name="by_cos", bufs=2)
+                by_sin[c] = ring.tile([P, B * N], F32, name="by_sin", bufs=2)
+            cols = slice(b * N, (b + 1) * N)
+            nc.vector.tensor_tensor(
+                out=by_cos[c][:, cols].rearrange("p (h d) -> p h d", h=HEADS),
+                in0=acc[c, b][:].rearrange("p (h d) -> p h d", h=HEADS),
+                in1=cos_sb[:].unsqueeze(1).to_broadcast([P, HEADS, DK]),
+                op=ALU.mult,
+            )
+            nc.vector.tensor_tensor(
+                out=by_sin[c][:, cols].rearrange("p (h j e) -> p h j e", h=HEADS, e=2),
+                in0=acc[c, b][:].rearrange("p (h j e) -> p h j e", h=HEADS, e=2)[:, :, :, ::-1],
+                in1=sin_signed[:].rearrange("p (j e) -> p j e", e=2).unsqueeze(1).to_broadcast([P, HEADS, DK // 2, 2]),
+                op=ALU.mult,
+            )
+
+        def add(engine, c, half, n0, n1):
+            if n0 == n1:
+                return
+            if (c, half) not in rotated:
+                if half == 1 and c + 2 < CHUNKS:
+                    rotated[c, half] = ring.tile([P, 2 * N], F32, name=shared_tag(c + 1), bufs=1, align_bytes=64)
+                else:
+                    rotated[c, half] = ring.tile([P, 2 * N], F32, name="rotated", bufs=3)
+            src = slice(half * 2 * N + n0, half * 2 * N + n1)
+            engine.tensor_tensor(
+                out=rotated[c, half][:, n0:n1], in0=by_cos[c][:, src], in1=by_sin[c][:, src], op=ALU.add
+            )
+
+        def store(c, b):
+            h0 = (c % CHUNKS_PER_W) * HEADS
+            nc.sync.dma_start(
+                out=outs[c // CHUNKS_PER_W][b, h0 : h0 + HEADS].rearrange("h s d -> s h d"),
+                in_=rotated[c, b // 2][:, (b % 2) * N : (b % 2 + 1) * N].rearrange("p (h d) -> p h d", h=HEADS),
+            )
+
+        def interleave_split(c, g, v_cols):
+            interleave("vector", c, g, 0, v_cols)
+            interleave("scalar", c, g, v_cols, N)
+
+        for g in range(PASSES):
+            load_w(0, g)
+            load_x(g)
+            if g == COS_AT:
+                nc.sync.dma_start(out=cos_sb[:], in_=cos2[:, :])
+                nc.sync.dma_start(out=sin_sb[:], in_=sin2[:, :])
+        for c in range(1, AHEAD + 1):
+            for g in range(PASSES):
+                load_w(c, g)
+
+        make_identity(nc, ident[:])
+        nc.gpsimd.tensor_scalar(
+            out=sin_signed[:, 0::2], in0=sin_sb[:, 0::2], scalar1=-1.0, scalar2=0.0, op0=ALU.mult, op1=ALU.add
+        )
+        nc.gpsimd.tensor_copy(out=sin_signed[:, 1::2], in_=sin_sb[:, 1::2])
+
+        for g in range(PASSES):
+            interleave_split(0, g, HEAD_V_COLS)
+            if g > 0:
+                quantize_x(g - 1)
+            quantize_w(0, g)
+            transpose_x(g)
+            copy_x(g)
+        interleave_split(1, 0, HEAD_V_COLS)
+        quantize_x(B - 1)
+        for b in range(B):
+            for g in range(PASSES):
+                multiply(0, g, b)
+
+        last = CHUNKS - 1
+        for c in range(CHUNKS):
+            if c > 0:
+                if c + AHEAD < CHUNKS:
+                    for g in range(PASSES):
+                        load_w(c + AHEAD, g)
+                quantize_w(c, 2)
+                quantize_w(c, 3)
+                add(nc.vector, c - 1, 0, 2 * N - V_ADD, 2 * N)
+                for b in range(2):
+                    store(c - 1, b)
+                for b in range(B):
+                    for g in range(2, PASSES):
+                        multiply(c, g, b)
+            if c < last:
+                if c > 0:
+                    interleave("scalar", c + 1, 0, 0, N)
+                interleave_split(c + 1, 1, V_COLS if c > 0 else HEAD_V_COLS)
+                quantize_w(c + 1, 0)
+                quantize_w(c + 1, 1)
+                interleave("scalar", c + 1, 2, 0, N)
+                interleave("scalar", c + 1, 3, 0, N)
+            if c > 0:
+                add(nc.gpsimd if c < last else nc.vector, c - 1, 1, 0, 2 * N)
+                for b in range(2, B):
+                    store(c - 1, b)
+            for b in range(B):
+                if c < last:
+                    for g in range(2):
+                        multiply(c + 1, g, b)
+                products(c, b)
+                if c < last and b == 1:
+                    add(nc.gpsimd, c, 0, 0, 2 * N - V_ADD)
+                if c == last:
+                    add(nc.gpsimd if b < B - 1 else nc.vector, c, b // 2, (b % 2) * N, (b % 2 + 1) * N)
+                    store(c, b)

@@ -22,10 +22,11 @@ CHUNKS_PER_W = E // N
 CHUNKS = 2 * CHUNKS_PER_W
 AHEAD = 3
 HEAD_V_COLS = 320
-V_COLS = 256
-V_ADD = 128
+V_COLS = 384
+V_ADD = 256
 ACC_BANKS = 5
-COS_AT = 1
+COS_AT = 0
+G_LAST = 2
 
 FLOPS = 2 * 2 * B * S * D * E
 
@@ -44,6 +45,7 @@ def tile_multiheadselfattention_pa_kernel(tc, x, Wq, Wk, cos2, sin2, out_0, out_
         ident = keep.tile([P, P], F32, name="ident")
         cos_sb = keep.tile([P, DK], BF16, name="cos_sb")
         sin_sb = keep.tile([P, DK], BF16, name="sin_sb")
+        signs = keep.tile([P, DK], F32, name="signs")
         sin_signed = keep.tile([P, DK], F32, name="sin_signed")
         x_codes = keep.tile([P, B, PASSES * S], U32, name="x_codes", align_bytes=64)
         x_scales = keep.tile([P, B, PASSES * S], U8, name="x_scales", align_bytes=64)
@@ -190,10 +192,9 @@ def tile_multiheadselfattention_pa_kernel(tc, x, Wq, Wk, cos2, sin2, out_0, out_
                 load_w(c, g)
 
         make_identity(nc, ident[:])
-        nc.gpsimd.tensor_scalar(
-            out=sin_signed[:, 0::2], in0=sin_sb[:, 0::2], scalar1=-1.0, scalar2=0.0, op0=ALU.mult, op1=ALU.add
-        )
-        nc.gpsimd.tensor_copy(out=sin_signed[:, 1::2], in_=sin_sb[:, 1::2])
+        nc.gpsimd.memset(signs[:], 1.0)
+        nc.gpsimd.memset(signs[:, 0::2], -1.0)
+        nc.gpsimd.tensor_tensor(out=sin_signed[:], in0=sin_sb[:], in1=signs[:], op=ALU.mult)
 
         for g in range(PASSES):
             interleave_split(0, g, HEAD_V_COLS)
@@ -241,6 +242,9 @@ def tile_multiheadselfattention_pa_kernel(tc, x, Wq, Wk, cos2, sin2, out_0, out_
                 products(c, b)
                 if c < last and b == 1:
                     add(nc.gpsimd, c, 0, 0, 2 * N - V_ADD)
-                if c == last:
-                    add(nc.gpsimd if b < B - 1 else nc.vector, c, b // 2, (b % 2) * N, (b % 2 + 1) * N)
+                if c == last and b < G_LAST:
+                    add(nc.gpsimd, c, b // 2, (b % 2) * N, (b % 2 + 1) * N)
                     store(c, b)
+        for b in range(G_LAST, B):
+            add(nc.vector, last, b // 2, (b % 2) * N, (b % 2 + 1) * N)
+            store(last, b)

@@ -20,13 +20,15 @@ N = 512
 HEADS = N // DK
 CHUNKS_PER_W = E // N
 CHUNKS = 2 * CHUNKS_PER_W
-AHEAD = 3
 HEAD_V_COLS = 320
-V_COLS = 384
-V_ADD = 256
+V_COLS = 320
+G_HEADS = 3
+W_BUFS = 8
+PAIR1 = 0
+TABLES_AT = 3
+TAIL = 2
+EARLY = 0
 ACC_BANKS = 5
-COS_AT = 0
-G_LAST = 2
 
 FLOPS = 2 * 2 * B * S * D * E
 
@@ -43,29 +45,41 @@ def tile_multiheadselfattention_pa_kernel(tc, x, Wq, Wk, cos2, sin2, out_0, out_
         ctx.enter_context(tc.manual_schedule())
 
         ident = keep.tile([P, P], F32, name="ident")
-        cos_sb = keep.tile([P, DK], BF16, name="cos_sb")
-        sin_sb = keep.tile([P, DK], BF16, name="sin_sb")
-        signs = keep.tile([P, DK], F32, name="signs")
-        sin_signed = keep.tile([P, DK], F32, name="sin_signed")
+        cos_sb = keep.tile([P, 2 * DK], BF16, name="cos_sb")
+        sin_sb = keep.tile([P, 2 * DK], BF16, name="sin_sb")
+        signs = keep.tile([P, 2 * DK], F32, name="signs")
+        sin_signed = keep.tile([P, 2 * DK], F32, name="sin_signed")
         x_codes = keep.tile([P, B, PASSES * S], U32, name="x_codes", align_bytes=64)
         x_scales = keep.tile([P, B, PASSES * S], U8, name="x_scales", align_bytes=64)
 
         x_raw, x_grouped, w_raw, w_grouped, w_codes, w_scales = {}, {}, {}, {}, {}, {}
+        w_pair = {}
         x_banks, acc, by_cos, by_sin, rotated = {}, {}, {}, {}, {}
 
         def bank(i):
             return psum.tile([P, N], F32, name="bank%d" % i)
 
         def load_x(b):
+            half, j = divmod(b, 2)
             x_raw[b] = keep.tile([P, D], BF16, name="x_raw%d" % b)
-            nc.sync.dma_start(out=x_raw[b][:], in_=x[b])
+            for r in range(2):
+                nc.sync.dma_start(out=x_raw[b][r:P:2, :], in_=x[2 * half + r, j:S:2, :])
 
-        def load_w(c, g):
+        def load_table(dst, table):
+            for r in range(2):
+                nc.sync.dma_start(out=dst[r:P:2, :], in_=table.rearrange("(q j) d -> q (j d)", j=2))
+
+        def load_w(c, g, chunks):
             w = weights[c // CHUNKS_PER_W]
             n0 = (c % CHUNKS_PER_W) * N
-            w_raw[c, g] = ring.tile([P, PACK, N], BF16, name="w_raw", bufs=(AHEAD + 1) * PASSES)
-            rows = w[g * K_PASS : (g + 1) * K_PASS, n0 : n0 + N]
-            nc.sync.dma_start(out=w_raw[c, g][:], in_=rows.rearrange("(p t) n -> p t n", t=PACK))
+            if c % 2 == 0:
+                w_pair[c // 2, g] = ring.tile([P, 2 * PACK * N], BF16, name="w_raw", bufs=W_BUFS)
+            span = slice((c % 2) * PACK * N, (c % 2 + chunks) * PACK * N)
+            dst = w_pair[c // 2, g][:, span].rearrange("p (t n) -> p t n", t=PACK)
+            rows = w[g * K_PASS : (g + 1) * K_PASS, n0 : n0 + chunks * N]
+            nc.sync.dma_start(out=dst, in_=rows.rearrange("(p t) n -> p t n", t=PACK))
+            for i in range(chunks):
+                w_raw[c + i, g] = dst[:, :, i * N : (i + 1) * N]
 
         def transpose_x(b):
             words = x_raw[b][:].bitcast(F32)
@@ -144,37 +158,45 @@ def tile_multiheadselfattention_pa_kernel(tc, x, Wq, Wk, cos2, sin2, out_0, out_
                 by_cos[c] = ring.tile([P, B * N], F32, name="by_cos", bufs=2)
                 by_sin[c] = ring.tile([P, B * N], F32, name="by_sin", bufs=2)
             cols = slice(b * N, (b + 1) * N)
+            table = slice((b % 2) * DK, (b % 2 + 1) * DK)
             nc.vector.tensor_tensor(
                 out=by_cos[c][:, cols].rearrange("p (h d) -> p h d", h=HEADS),
                 in0=acc[c, b][:].rearrange("p (h d) -> p h d", h=HEADS),
-                in1=cos_sb[:].unsqueeze(1).to_broadcast([P, HEADS, DK]),
+                in1=cos_sb[:, table].unsqueeze(1).to_broadcast([P, HEADS, DK]),
                 op=ALU.mult,
             )
             nc.vector.tensor_tensor(
-                out=by_sin[c][:, cols].rearrange("p (h j e) -> p h j e", h=HEADS, e=2),
-                in0=acc[c, b][:].rearrange("p (h j e) -> p h j e", h=HEADS, e=2)[:, :, :, ::-1],
-                in1=sin_signed[:].rearrange("p (j e) -> p j e", e=2).unsqueeze(1).to_broadcast([P, HEADS, DK // 2, 2]),
+                out=by_sin[c][:, cols].rearrange("p (h m e) -> p h m e", h=HEADS, e=2),
+                in0=acc[c, b][:].rearrange("p (h m e) -> p h m e", h=HEADS, e=2)[:, :, :, ::-1],
+                in1=sin_signed[:, table]
+                .rearrange("p (m e) -> p m e", e=2)
+                .unsqueeze(1)
+                .to_broadcast([P, HEADS, DK // 2, 2]),
                 op=ALU.mult,
             )
 
-        def add(engine, c, half, n0, n1):
-            if n0 == n1:
-                return
+        def open_rotated(c, half):
+            if half == 1 and c + 2 < CHUNKS:
+                rotated[c, half] = ring.tile([P, 2 * N], F32, name=shared_tag(c + 1), bufs=1, align_bytes=64)
+            else:
+                rotated[c, half] = ring.tile([P, 2 * N], F32, name="rotated", bufs=3)
+
+        def add(engine, c, half, heads, rows):
             if (c, half) not in rotated:
-                if half == 1 and c + 2 < CHUNKS:
-                    rotated[c, half] = ring.tile([P, 2 * N], F32, name=shared_tag(c + 1), bufs=1, align_bytes=64)
-                else:
-                    rotated[c, half] = ring.tile([P, 2 * N], F32, name="rotated", bufs=3)
-            src = slice(half * 2 * N + n0, half * 2 * N + n1)
+                open_rotated(c, half)
+            src = slice(half * 2 * N, (half + 1) * 2 * N)
             engine.tensor_tensor(
-                out=rotated[c, half][:, n0:n1], in0=by_cos[c][:, src], in1=by_sin[c][:, src], op=ALU.add
+                out=rotated[c, half][:].rearrange("p (h j d) -> p h j d", h=HEADS, j=2)[:, heads, rows, :],
+                in0=by_cos[c][:, src].rearrange("p (j h d) -> p h j d", h=HEADS, j=2)[:, heads, rows, :],
+                in1=by_sin[c][:, src].rearrange("p (j h d) -> p h j d", h=HEADS, j=2)[:, heads, rows, :],
+                op=ALU.add,
             )
 
-        def store(c, b):
+        def store(c, b, heads=slice(0, HEADS)):
             h0 = (c % CHUNKS_PER_W) * HEADS
             nc.sync.dma_start(
-                out=outs[c // CHUNKS_PER_W][b, h0 : h0 + HEADS].rearrange("h s d -> s h d"),
-                in_=rotated[c, b // 2][:, (b % 2) * N : (b % 2 + 1) * N].rearrange("p (h d) -> p h d", h=HEADS),
+                out=outs[c // CHUNKS_PER_W][b, h0 + heads.start : h0 + heads.stop].rearrange("h (q j) d -> q h (j d)", j=2),
+                in_=rotated[c, b // 2][b % 2 : P : 2, :].rearrange("p (h e) -> p h e", h=HEADS)[:, heads, :],
             )
 
         def interleave_split(c, g, v_cols):
@@ -182,19 +204,24 @@ def tile_multiheadselfattention_pa_kernel(tc, x, Wq, Wk, cos2, sin2, out_0, out_
             interleave("scalar", c, g, v_cols, N)
 
         for g in range(PASSES):
-            load_w(0, g)
+            load_w(0, g, 1)
             load_x(g)
-            if g == COS_AT:
-                nc.sync.dma_start(out=cos_sb[:], in_=cos2[:, :])
-                nc.sync.dma_start(out=sin_sb[:], in_=sin2[:, :])
-        for c in range(1, AHEAD + 1):
+            if g == TABLES_AT:
+                load_table(cos_sb, cos2)
+                load_table(sin_sb, sin2)
+        for g in range(PASSES):
+            load_w(1, g, 1)
+        if PAIR1:
             for g in range(PASSES):
-                load_w(c, g)
+                load_w(2, g, 2)
+        else:
+            for c in (2, 3):
+                for g in range(PASSES):
+                    load_w(c, g, 1)
 
         make_identity(nc, ident[:])
         nc.gpsimd.memset(signs[:], 1.0)
         nc.gpsimd.memset(signs[:, 0::2], -1.0)
-        nc.gpsimd.tensor_tensor(out=sin_signed[:], in0=sin_sb[:], in1=signs[:], op=ALU.mult)
 
         for g in range(PASSES):
             interleave_split(0, g, HEAD_V_COLS)
@@ -203,6 +230,7 @@ def tile_multiheadselfattention_pa_kernel(tc, x, Wq, Wk, cos2, sin2, out_0, out_
             quantize_w(0, g)
             transpose_x(g)
             copy_x(g)
+        nc.vector.tensor_tensor(out=sin_signed[:], in0=sin_sb[:], in1=signs[:], op=ALU.mult)
         interleave_split(1, 0, HEAD_V_COLS)
         quantize_x(B - 1)
         for b in range(B):
@@ -210,14 +238,15 @@ def tile_multiheadselfattention_pa_kernel(tc, x, Wq, Wk, cos2, sin2, out_0, out_
                 multiply(0, g, b)
 
         last = CHUNKS - 1
+        both = slice(0, 2)
         for c in range(CHUNKS):
             if c > 0:
-                if c + AHEAD < CHUNKS:
+                if c in (1, 3):
                     for g in range(PASSES):
-                        load_w(c + AHEAD, g)
+                        load_w(c + 3, g, 2)
                 quantize_w(c, 2)
                 quantize_w(c, 3)
-                add(nc.vector, c - 1, 0, 2 * N - V_ADD, 2 * N)
+                add(nc.vector, c - 1, 0, slice(G_HEADS, HEADS), both)
                 for b in range(2):
                     store(c - 1, b)
                 for b in range(B):
@@ -232,7 +261,7 @@ def tile_multiheadselfattention_pa_kernel(tc, x, Wq, Wk, cos2, sin2, out_0, out_
                 interleave("scalar", c + 1, 2, 0, N)
                 interleave("scalar", c + 1, 3, 0, N)
             if c > 0:
-                add(nc.gpsimd if c < last else nc.vector, c - 1, 1, 0, 2 * N)
+                add(nc.gpsimd if c < last else nc.vector, c - 1, 1, slice(0, HEADS), both)
                 for b in range(2, B):
                     store(c - 1, b)
             for b in range(B):
@@ -241,10 +270,12 @@ def tile_multiheadselfattention_pa_kernel(tc, x, Wq, Wk, cos2, sin2, out_0, out_
                         multiply(c + 1, g, b)
                 products(c, b)
                 if c < last and b == 1:
-                    add(nc.gpsimd, c, 0, 0, 2 * N - V_ADD)
-                if c == last and b < G_LAST:
-                    add(nc.gpsimd, c, b // 2, (b % 2) * N, (b % 2 + 1) * N)
-                    store(c, b)
-        for b in range(G_LAST, B):
-            add(nc.vector, last, b // 2, (b % 2) * N, (b % 2 + 1) * N)
+                    add(nc.gpsimd, c, 0, slice(0, G_HEADS), both)
+                if c == last and b < 2:
+                    add(nc.gpsimd, c, 0, slice(0, HEADS), slice(b, b + 1))
+        for b in range(2):
             store(last, b)
+        for h0 in range(0, HEADS, TAIL):
+            add(nc.vector, last, 1, slice(h0, h0 + TAIL), both)
+            for b in range(2, B):
+                store(last, b, slice(h0, h0 + TAIL))

@@ -17,18 +17,14 @@ PACK = 4
 K_PASS = P * PACK
 PASSES = D // K_PASS
 N = 512
-HEADS = N // DK
-CHUNKS_PER_W = E // N
-CHUNKS = 2 * CHUNKS_PER_W
-HEAD_V_COLS = 320
-V_COLS = 320
-G_HEADS = 3
-W_BUFS = 8
-PAIR1 = 0
-TABLES_AT = 3
-TAIL = 2
-EARLY = 0
+GROUPS = 4
 ACC_BANKS = 5
+HEAD_V_COLS = 320
+V_COLS = 256
+V_LAST = 0
+V_HEADS = 1
+SPLIT = 1
+G_TAIL = 1
 
 FLOPS = 2 * 2 * B * S * D * E
 
@@ -37,6 +33,10 @@ def tile_multiheadselfattention_pa_kernel(tc, x, Wq, Wk, cos2, sin2, out_0, out_
     nc = tc.nc
     weights = (Wq, Wk)
     outs = (out_0, out_1)
+    chunks = [(m, n0, N) for m in range(2) for n0 in range(0, E, N)]
+    if SPLIT:
+        chunks = chunks[:-1] + [(1, E - N, N // 2), (1, E - N // 2, N // 2)]
+    last = len(chunks) - 1
 
     with ExitStack() as ctx:
         keep = ctx.enter_context(tc.tile_pool(name="keep", bufs=1))
@@ -49,233 +49,212 @@ def tile_multiheadselfattention_pa_kernel(tc, x, Wq, Wk, cos2, sin2, out_0, out_
         sin_sb = keep.tile([P, 2 * DK], BF16, name="sin_sb")
         signs = keep.tile([P, 2 * DK], F32, name="signs")
         sin_signed = keep.tile([P, 2 * DK], F32, name="sin_signed")
-        x_codes = keep.tile([P, B, PASSES * S], U32, name="x_codes", align_bytes=64)
-        x_scales = keep.tile([P, B, PASSES * S], U8, name="x_scales", align_bytes=64)
+        x_codes = keep.tile([P, GROUPS, PASSES * P], U32, name="x_codes", align_bytes=64)
+        x_scales = keep.tile([P, GROUPS, PASSES * P], U8, name="x_scales", align_bytes=64)
 
-        x_raw, x_grouped, w_raw, w_grouped, w_codes, w_scales = {}, {}, {}, {}, {}, {}
-        w_pair = {}
-        x_banks, acc, by_cos, by_sin, rotated = {}, {}, {}, {}, {}
+        x_raw, x_banks, x_grouped = {}, {}, {}
+        w_slot, w_raw, w_grouped, w_codes, w_scales = {}, {}, {}, {}, {}
+        acc, by_cos, by_sin, rotated = {}, {}, {}, {}
 
         def bank(i):
             return psum.tile([P, N], F32, name="bank%d" % i)
 
-        def load_x(b):
-            half, j = divmod(b, 2)
-            x_raw[b] = keep.tile([P, D], BF16, name="x_raw%d" % b)
+        def width(c):
+            return chunks[c][2]
+
+        def heads(c):
+            return width(c) // DK
+
+        def load_x(t):
+            half, j = divmod(t, 2)
+            x_raw[t] = keep.tile([P, D], BF16, name="x_raw%d" % t)
             for r in range(2):
-                nc.sync.dma_start(out=x_raw[b][r:P:2, :], in_=x[2 * half + r, j:S:2, :])
+                nc.sync.dma_start(out=x_raw[t][r:P:2, :], in_=x[2 * half + r, j:S:2, :])
 
         def load_table(dst, table):
             for r in range(2):
                 nc.sync.dma_start(out=dst[r:P:2, :], in_=table.rearrange("(q j) d -> q (j d)", j=2))
 
-        def load_w(c, g, chunks):
-            w = weights[c // CHUNKS_PER_W]
-            n0 = (c % CHUNKS_PER_W) * N
-            if c % 2 == 0:
-                w_pair[c // 2, g] = ring.tile([P, 2 * PACK * N], BF16, name="w_raw", bufs=W_BUFS)
-            span = slice((c % 2) * PACK * N, (c % 2 + chunks) * PACK * N)
-            dst = w_pair[c // 2, g][:, span].rearrange("p (t n) -> p t n", t=PACK)
-            rows = w[g * K_PASS : (g + 1) * K_PASS, n0 : n0 + chunks * N]
+        def load_w(m, n0, cols, g):
+            if n0 % (2 * N) == 0:
+                w_slot[m, g] = ring.tile([P, 2 * PACK * N], BF16, name="w_raw", bufs=2 * PASSES)
+            start = PACK * (n0 % (2 * N))
+            dst = w_slot[m, g][:, start : start + PACK * cols].rearrange("p (t n) -> p t n", t=PACK)
+            rows = weights[m][g * K_PASS : (g + 1) * K_PASS, n0 : n0 + cols]
             nc.sync.dma_start(out=dst, in_=rows.rearrange("(p t) n -> p t n", t=PACK))
-            for i in range(chunks):
-                w_raw[c + i, g] = dst[:, :, i * N : (i + 1) * N]
+            for c, (cm, cn, cw) in enumerate(chunks):
+                if cm == m and n0 <= cn < n0 + cols:
+                    w_raw[c, g] = dst[:, :, cn - n0 : cn - n0 + cw]
 
-        def transpose_x(b):
-            words = x_raw[b][:].bitcast(F32)
-            for half in range(2):
-                xt = bank(4 + 2 * (b % 2) + half)
-                x_banks[b, half] = xt
-                for gg in range(2):
-                    g = 2 * half + gg
-                    for u in range(2):
-                        col = (2 * gg + u) * S
-                        nc.tensor.transpose(
-                            xt[:, col : col + S], words[:, 256 * g + u : 256 * (g + 1) : 2], ident[:]
-                        )
+        def transpose_x(t):
+            words = x_raw[t][:].bitcast(F32)
+            for pair in range(PASSES // 2):
+                x_banks[t, pair] = bank(4 + 2 * (t % 2) + pair)
+                for i in range(4):
+                    g, u = 2 * pair + i // 2, i % 2
+                    nc.tensor.transpose(
+                        x_banks[t, pair][:, i * P : (i + 1) * P], words[:, 256 * g + u : 256 * (g + 1) : 2], ident[:]
+                    )
 
-        def copy_x(b):
-            x_grouped[b] = ring.tile([P, D], BF16, name="x_grouped", bufs=2, align_bytes=64)
-            words = x_grouped[b][:].bitcast(F32)
-            for half in range(2):
+        def copy_x(t):
+            x_grouped[t] = ring.tile([P, D], BF16, name="x_grouped", bufs=2, align_bytes=64)
+            words = x_grouped[t][:].bitcast(F32)
+            for pair in range(PASSES // 2):
                 nc.scalar.copy(
-                    out=words[:, half * N : (half + 1) * N].rearrange("p (g s u) -> p g s u", g=2, u=2),
-                    in_=x_banks[b, half][:].rearrange("p (g u s) -> p g s u", g=2, u=2),
+                    out=words[:, pair * N : (pair + 1) * N].rearrange("p (g s u) -> p g s u", g=2, u=2),
+                    in_=x_banks[t, pair][:].rearrange("p (g u s) -> p g s u", g=2, u=2),
                 )
 
-        def quantize_x(b):
+        def quantize_x(t):
             nc.vector.quantize_mx(
-                out=x_codes[:, b, :].bitcast(FP8X4), scales=x_scales[:, b, :], in_=x_grouped[b][:]
+                out=x_codes[:, t, :].bitcast(FP8X4), scales=x_scales[:, t, :], in_=x_grouped[t][:]
             )
 
-        def last_before_rotation(c):
-            return (c + 1, 1)
+        def shared_tile(c, shape, dtype):
+            return ring.tile(shape, dtype, name="shared%d" % (c % 3), bufs=1, align_bytes=64)
 
-        def shared_tag(c):
-            return "shared%d" % (c % 3)
-
-        def interleave(engine, c, g, n0, n1):
-            if n0 == n1:
-                return
-            if (c, g) not in w_grouped:
-                holders = [cc for cc in range(1, CHUNKS) if last_before_rotation(cc) == (c, g)]
-                if holders:
-                    w_grouped[c, g] = ring.tile([P, N, PACK], BF16, name=shared_tag(holders[0]), bufs=1, align_bytes=64)
-                else:
-                    w_grouped[c, g] = ring.tile([P, N, PACK], BF16, name="w_grouped", bufs=7, align_bytes=64)
-            dst = w_grouped[c, g][:, n0:n1, :].rearrange("p (n i) t -> p n t i", i=4)
-            src = w_raw[c, g][:, :, n0:n1].rearrange("p t (n i) -> p n t i", i=4)
-            if engine == "vector":
-                nc.vector.tensor_copy(out=dst, in_=src)
+        def interleave(c, g, v_cols):
+            if g == 1 and c >= 2:
+                w_grouped[c, g] = shared_tile(c, [P, width(c), PACK], BF16)
             else:
-                nc.scalar.copy(out=dst, in_=src)
+                w_grouped[c, g] = ring.tile([P, width(c), PACK], BF16, name="w_grouped", bufs=7, align_bytes=64)
+            dst = w_grouped[c, g][:].rearrange("p (n i) t -> p n t i", i=4)
+            src = w_raw[c, g].rearrange("p t (n i) -> p n t i", i=4)
+            cut = v_cols // 4
+            if cut > 0:
+                nc.vector.tensor_copy(out=dst[:, :cut], in_=src[:, :cut])
+            if v_cols < width(c):
+                nc.scalar.copy(out=dst[:, cut:], in_=src[:, cut:])
 
         def quantize_w(c, g):
-            w_codes[c, g] = ring.tile([P, N], U32, name="w_codes", bufs=8, align_bytes=64)
-            w_scales[c, g] = ring.tile([P, N], U8, name="w_scales", bufs=8, align_bytes=64)
+            w_codes[c, g] = ring.tile([P, width(c)], U32, name="w_codes", bufs=8, align_bytes=64)
+            w_scales[c, g] = ring.tile([P, width(c)], U8, name="w_scales", bufs=8, align_bytes=64)
             nc.vector.quantize_mx(
                 out=w_codes[c, g][:].bitcast(FP8X4),
                 scales=w_scales[c, g][:],
                 in_=w_grouped[c, g][:].rearrange("p n t -> p (n t)"),
             )
 
-        def multiply(c, g, b):
-            if g == 0:
-                acc[c, b] = bank((B * c + b) % ACC_BANKS)
-            cols = slice(g * S, (g + 1) * S)
-            nc.tensor.matmul_mx(
-                out=acc[c, b][:],
-                lhsT=x_codes[:, b, cols].bitcast(FP8X4),
-                lhsT_scale=x_scales[:, b, cols],
-                rhs=w_codes[c, g][:].bitcast(FP8X4),
-                rhs_scale=w_scales[c, g][:],
-                start=(g == 0),
-                stop=(g == PASSES - 1),
-            )
+        def multiply(c, t, passes):
+            for g in passes:
+                if g == 0:
+                    acc[c, t] = bank((GROUPS * c + t) % ACC_BANKS)[:, : width(c)]
+                cols = slice(g * P, (g + 1) * P)
+                nc.tensor.matmul_mx(
+                    out=acc[c, t],
+                    lhsT=x_codes[:, t, cols].bitcast(FP8X4),
+                    lhsT_scale=x_scales[:, t, cols],
+                    rhs=w_codes[c, g][:].bitcast(FP8X4),
+                    rhs_scale=w_scales[c, g][:],
+                    start=(g == 0),
+                    stop=(g == PASSES - 1),
+                )
 
-        def products(c, b):
-            if b == 0:
-                by_cos[c] = ring.tile([P, B * N], F32, name="by_cos", bufs=2)
-                by_sin[c] = ring.tile([P, B * N], F32, name="by_sin", bufs=2)
-            cols = slice(b * N, (b + 1) * N)
-            table = slice((b % 2) * DK, (b % 2 + 1) * DK)
+        def products(c, t):
+            if t == 0:
+                by_cos[c] = ring.tile([P, GROUPS, width(c)], F32, name="by_cos", bufs=2)
+                by_sin[c] = ring.tile([P, GROUPS, width(c)], F32, name="by_sin", bufs=2)
+            table = slice((t % 2) * DK, (t % 2 + 1) * DK)
             nc.vector.tensor_tensor(
-                out=by_cos[c][:, cols].rearrange("p (h d) -> p h d", h=HEADS),
-                in0=acc[c, b][:].rearrange("p (h d) -> p h d", h=HEADS),
-                in1=cos_sb[:, table].unsqueeze(1).to_broadcast([P, HEADS, DK]),
+                out=by_cos[c][:, t, :].rearrange("p (h d) -> p h d", d=DK),
+                in0=acc[c, t].rearrange("p (h d) -> p h d", d=DK),
+                in1=cos_sb[:, table].unsqueeze(1).to_broadcast([P, heads(c), DK]),
                 op=ALU.mult,
             )
             nc.vector.tensor_tensor(
-                out=by_sin[c][:, cols].rearrange("p (h m e) -> p h m e", h=HEADS, e=2),
-                in0=acc[c, b][:].rearrange("p (h m e) -> p h m e", h=HEADS, e=2)[:, :, :, ::-1],
+                out=by_sin[c][:, t, :].rearrange("p (h m e) -> p h m e", m=DK // 2, e=2),
+                in0=acc[c, t].rearrange("p (h m e) -> p h m e", m=DK // 2, e=2)[:, :, :, ::-1],
                 in1=sin_signed[:, table]
                 .rearrange("p (m e) -> p m e", e=2)
                 .unsqueeze(1)
-                .to_broadcast([P, HEADS, DK // 2, 2]),
+                .to_broadcast([P, heads(c), DK // 2, 2]),
                 op=ALU.mult,
             )
 
-        def open_rotated(c, half):
-            if half == 1 and c + 2 < CHUNKS:
-                rotated[c, half] = ring.tile([P, 2 * N], F32, name=shared_tag(c + 1), bufs=1, align_bytes=64)
-            else:
-                rotated[c, half] = ring.tile([P, 2 * N], F32, name="rotated", bufs=3)
-
-        def add(engine, c, half, heads, rows):
+        def add(engine, c, half, h0, h1, rows=slice(0, 2)):
+            if h0 == h1:
+                return
             if (c, half) not in rotated:
-                open_rotated(c, half)
-            src = slice(half * 2 * N, (half + 1) * 2 * N)
+                if half == 1 and c + 2 <= last:
+                    rotated[c, half] = shared_tile(c + 2, [P, heads(c), 2, DK], F32)
+                else:
+                    rotated[c, half] = ring.tile([P, heads(c), 2, DK], F32, name="rotated", bufs=3)
+            pair = slice(2 * half, 2 * half + 2)
             engine.tensor_tensor(
-                out=rotated[c, half][:].rearrange("p (h j d) -> p h j d", h=HEADS, j=2)[:, heads, rows, :],
-                in0=by_cos[c][:, src].rearrange("p (j h d) -> p h j d", h=HEADS, j=2)[:, heads, rows, :],
-                in1=by_sin[c][:, src].rearrange("p (j h d) -> p h j d", h=HEADS, j=2)[:, heads, rows, :],
+                out=rotated[c, half][:, h0:h1, rows, :],
+                in0=by_cos[c][:, pair, :].rearrange("p j (h d) -> p h j d", d=DK)[:, h0:h1, rows, :],
+                in1=by_sin[c][:, pair, :].rearrange("p j (h d) -> p h j d", d=DK)[:, h0:h1, rows, :],
                 op=ALU.add,
             )
 
-        def store(c, b, heads=slice(0, HEADS)):
-            h0 = (c % CHUNKS_PER_W) * HEADS
-            nc.sync.dma_start(
-                out=outs[c // CHUNKS_PER_W][b, h0 + heads.start : h0 + heads.stop].rearrange("h (q j) d -> q h (j d)", j=2),
-                in_=rotated[c, b // 2][b % 2 : P : 2, :].rearrange("p (h e) -> p h e", h=HEADS)[:, heads, :],
-            )
+        def store(c, half, h0, h1):
+            m, n0, cw = chunks[c]
+            for r in range(2):
+                nc.sync.dma_start(
+                    out=outs[m][2 * half + r, n0 // DK + h0 : n0 // DK + h1].rearrange("h (q j) d -> q h (j d)", j=2),
+                    in_=rotated[c, half][r:P:2, h0:h1].rearrange("p h j d -> p h (j d)"),
+                )
 
-        def interleave_split(c, g, v_cols):
-            interleave("vector", c, g, 0, v_cols)
-            interleave("scalar", c, g, v_cols, N)
+        def gpsimd_heads(c):
+            return heads(c) - V_HEADS if width(c) == N else 0
 
         for g in range(PASSES):
-            load_w(0, g, 1)
+            load_w(0, 0, N, g)
             load_x(g)
-            if g == TABLES_AT:
-                load_table(cos_sb, cos2)
-                load_table(sin_sb, sin2)
-        for g in range(PASSES):
-            load_w(1, g, 1)
-        if PAIR1:
+        load_table(cos_sb, cos2)
+        load_table(sin_sb, sin2)
+        for n0 in range(N, E, N):
             for g in range(PASSES):
-                load_w(2, g, 2)
-        else:
-            for c in (2, 3):
-                for g in range(PASSES):
-                    load_w(c, g, 1)
+                load_w(0, n0, N, g)
 
         make_identity(nc, ident[:])
         nc.gpsimd.memset(signs[:], 1.0)
         nc.gpsimd.memset(signs[:, 0::2], -1.0)
 
         for g in range(PASSES):
-            interleave_split(0, g, HEAD_V_COLS)
+            interleave(0, g, HEAD_V_COLS)
             if g > 0:
                 quantize_x(g - 1)
             quantize_w(0, g)
             transpose_x(g)
             copy_x(g)
         nc.vector.tensor_tensor(out=sin_signed[:], in0=sin_sb[:], in1=signs[:], op=ALU.mult)
-        interleave_split(1, 0, HEAD_V_COLS)
-        quantize_x(B - 1)
-        for b in range(B):
-            for g in range(PASSES):
-                multiply(0, g, b)
+        interleave(1, 0, HEAD_V_COLS)
+        quantize_x(GROUPS - 1)
+        for t in range(GROUPS):
+            multiply(0, t, range(PASSES))
 
-        last = CHUNKS - 1
-        both = slice(0, 2)
-        for c in range(CHUNKS):
+        for c in range(last + 1):
+            if c in (1, 3):
+                for g in range(PASSES):
+                    load_w(1, (c - 1) * N, 2 * N, g)
             if c > 0:
-                if c in (1, 3):
-                    for g in range(PASSES):
-                        load_w(c + 3, g, 2)
                 quantize_w(c, 2)
                 quantize_w(c, 3)
-                add(nc.vector, c - 1, 0, slice(G_HEADS, HEADS), both)
-                for b in range(2):
-                    store(c - 1, b)
-                for b in range(B):
-                    for g in range(2, PASSES):
-                        multiply(c, g, b)
+                add(nc.vector, c - 1, 0, gpsimd_heads(c - 1), heads(c - 1))
+                store(c - 1, 0, 0, heads(c - 1))
+                for t in range(GROUPS):
+                    multiply(c, t, (2, 3))
             if c < last:
                 if c > 0:
-                    interleave("scalar", c + 1, 0, 0, N)
-                interleave_split(c + 1, 1, V_COLS if c > 0 else HEAD_V_COLS)
+                    interleave(c + 1, 0, 0)
+                interleave(c + 1, 1, HEAD_V_COLS if c == 0 else V_COLS if width(c + 1) == N else V_LAST)
                 quantize_w(c + 1, 0)
                 quantize_w(c + 1, 1)
-                interleave("scalar", c + 1, 2, 0, N)
-                interleave("scalar", c + 1, 3, 0, N)
+                interleave(c + 1, 2, 0)
+                interleave(c + 1, 3, 0)
             if c > 0:
-                add(nc.gpsimd if c < last else nc.vector, c - 1, 1, slice(0, HEADS), both)
-                for b in range(2, B):
-                    store(c - 1, b)
-            for b in range(B):
+                add(nc.gpsimd if c < last else nc.vector, c - 1, 1, 0, heads(c - 1))
+                store(c - 1, 1, 0, heads(c - 1))
+            for t in range(GROUPS):
                 if c < last:
-                    for g in range(2):
-                        multiply(c + 1, g, b)
-                products(c, b)
-                if c < last and b == 1:
-                    add(nc.gpsimd, c, 0, slice(0, G_HEADS), both)
-                if c == last and b < 2:
-                    add(nc.gpsimd, c, 0, slice(0, HEADS), slice(b, b + 1))
-        for b in range(2):
-            store(last, b)
-        for h0 in range(0, HEADS, TAIL):
-            add(nc.vector, last, 1, slice(h0, h0 + TAIL), both)
-            for b in range(2, B):
-                store(last, b, slice(h0, h0 + TAIL))
+                    multiply(c + 1, t, (0, 1))
+                products(c, t)
+                if c < last and t == 1:
+                    add(nc.gpsimd, c, 0, 0, gpsimd_heads(c))
+                if c == last and t < 2:
+                    add(nc.gpsimd, c, 0, 0, heads(c), slice(t, t + 1))
+        store(last, 0, 0, heads(last))
+        for h0 in range(0, heads(last), G_TAIL):
+            add(nc.vector, last, 1, h0, h0 + G_TAIL)
+            store(last, 1, h0, h0 + G_TAIL)

from contextlib import ExitStack

import concourse.mybir as mybir
from concourse.masks import make_identity

F32 = mybir.dt.float32
BF16 = mybir.dt.bfloat16
U32 = mybir.dt.uint32
U8 = mybir.dt.uint8
FP8X4 = mybir.dt.float8_e5m2_x4
ALU = mybir.AluOpType

B, S, D, H, DK = 4, 128, 2048, 16, 128
E = H * DK
P = 128
PACK = 4
K_PASS = P * PACK
PASSES = D // K_PASS
N = 512
GROUPS = 4
ACC_BANKS = 5
HEAD_V_COLS = 320
V_COLS = 256
V_LAST = 0
V_HEADS = 1
SPLIT = 1
G_TAIL = 1

FLOPS = 2 * 2 * B * S * D * E


def tile_multiheadselfattention_pa_kernel(tc, x, Wq, Wk, cos2, sin2, out_0, out_1):
    nc = tc.nc
    weights = (Wq, Wk)
    outs = (out_0, out_1)
    chunks = [(m, n0, N) for m in range(2) for n0 in range(0, E, N)]
    if SPLIT:
        chunks = chunks[:-1] + [(1, E - N, N // 2), (1, E - N // 2, N // 2)]
    last = len(chunks) - 1

    with ExitStack() as ctx:
        keep = ctx.enter_context(tc.tile_pool(name="keep", bufs=1))
        ring = ctx.enter_context(tc.tile_pool(name="ring", bufs=2))
        psum = ctx.enter_context(tc.psum_pool(name="psum", bufs=1))
        ctx.enter_context(tc.manual_schedule())

        ident = keep.tile([P, P], F32, name="ident")
        cos_sb = keep.tile([P, 2 * DK], BF16, name="cos_sb")
        sin_sb = keep.tile([P, 2 * DK], BF16, name="sin_sb")
        signs = keep.tile([P, 2 * DK], F32, name="signs")
        sin_signed = keep.tile([P, 2 * DK], F32, name="sin_signed")
        x_codes = keep.tile([P, GROUPS, PASSES * P], U32, name="x_codes", align_bytes=64)
        x_scales = keep.tile([P, GROUPS, PASSES * P], U8, name="x_scales", align_bytes=64)

        x_raw, x_banks, x_grouped = {}, {}, {}
        w_slot, w_raw, w_grouped, w_codes, w_scales = {}, {}, {}, {}, {}
        acc, by_cos, by_sin, rotated = {}, {}, {}, {}

        def bank(i):
            return psum.tile([P, N], F32, name="bank%d" % i)

        def width(c):
            return chunks[c][2]

        def heads(c):
            return width(c) // DK

        def load_x(t):
            half, j = divmod(t, 2)
            x_raw[t] = keep.tile([P, D], BF16, name="x_raw%d" % t)
            for r in range(2):
                nc.sync.dma_start(out=x_raw[t][r:P:2, :], in_=x[2 * half + r, j:S:2, :])

        def load_table(dst, table):
            for r in range(2):
                nc.sync.dma_start(out=dst[r:P:2, :], in_=table.rearrange("(q j) d -> q (j d)", j=2))

        def load_w(m, n0, cols, g):
            if n0 % (2 * N) == 0:
                w_slot[m, g] = ring.tile([P, 2 * PACK * N], BF16, name="w_raw", bufs=2 * PASSES)
            start = PACK * (n0 % (2 * N))
            dst = w_slot[m, g][:, start : start + PACK * cols].rearrange("p (t n) -> p t n", t=PACK)
            rows = weights[m][g * K_PASS : (g + 1) * K_PASS, n0 : n0 + cols]
            nc.sync.dma_start(out=dst, in_=rows.rearrange("(p t) n -> p t n", t=PACK))
            for c, (cm, cn, cw) in enumerate(chunks):
                if cm == m and n0 <= cn < n0 + cols:
                    w_raw[c, g] = dst[:, :, cn - n0 : cn - n0 + cw]

        def transpose_x(t):
            words = x_raw[t][:].bitcast(F32)
            for pair in range(PASSES // 2):
                x_banks[t, pair] = bank(4 + 2 * (t % 2) + pair)
                for i in range(4):
                    g, u = 2 * pair + i // 2, i % 2
                    nc.tensor.transpose(
                        x_banks[t, pair][:, i * P : (i + 1) * P], words[:, 256 * g + u : 256 * (g + 1) : 2], ident[:]
                    )

        def copy_x(t):
            x_grouped[t] = ring.tile([P, D], BF16, name="x_grouped", bufs=2, align_bytes=64)
            words = x_grouped[t][:].bitcast(F32)
            for pair in range(PASSES // 2):
                nc.scalar.copy(
                    out=words[:, pair * N : (pair + 1) * N].rearrange("p (g s u) -> p g s u", g=2, u=2),
                    in_=x_banks[t, pair][:].rearrange("p (g u s) -> p g s u", g=2, u=2),
                )

        def quantize_x(t):
            nc.vector.quantize_mx(
                out=x_codes[:, t, :].bitcast(FP8X4), scales=x_scales[:, t, :], in_=x_grouped[t][:]
            )

        def shared_tile(c, shape, dtype):
            return ring.tile(shape, dtype, name="shared%d" % (c % 3), bufs=1, align_bytes=64)

        def interleave(c, g, v_cols):
            if g == 1 and c >= 2:
                w_grouped[c, g] = shared_tile(c, [P, width(c), PACK], BF16)
            else:
                w_grouped[c, g] = ring.tile([P, width(c), PACK], BF16, name="w_grouped", bufs=7, align_bytes=64)
            dst = w_grouped[c, g][:].rearrange("p (n i) t -> p n t i", i=4)
            src = w_raw[c, g].rearrange("p t (n i) -> p n t i", i=4)
            cut = v_cols // 4
            if cut > 0:
                nc.vector.tensor_copy(out=dst[:, :cut], in_=src[:, :cut])
            if v_cols < width(c):
                nc.scalar.copy(out=dst[:, cut:], in_=src[:, cut:])

        def quantize_w(c, g):
            w_codes[c, g] = ring.tile([P, width(c)], U32, name="w_codes", bufs=8, align_bytes=64)
            w_scales[c, g] = ring.tile([P, width(c)], U8, name="w_scales", bufs=8, align_bytes=64)
            nc.vector.quantize_mx(
                out=w_codes[c, g][:].bitcast(FP8X4),
                scales=w_scales[c, g][:],
                in_=w_grouped[c, g][:].rearrange("p n t -> p (n t)"),
            )

        def multiply(c, t, passes):
            for g in passes:
                if g == 0:
                    acc[c, t] = bank((GROUPS * c + t) % ACC_BANKS)[:, : width(c)]
                cols = slice(g * P, (g + 1) * P)
                nc.tensor.matmul_mx(
                    out=acc[c, t],
                    lhsT=x_codes[:, t, cols].bitcast(FP8X4),
                    lhsT_scale=x_scales[:, t, cols],
                    rhs=w_codes[c, g][:].bitcast(FP8X4),
                    rhs_scale=w_scales[c, g][:],
                    start=(g == 0),
                    stop=(g == PASSES - 1),
                )

        def products(c, t):
            if t == 0:
                by_cos[c] = ring.tile([P, GROUPS, width(c)], F32, name="by_cos", bufs=2)
                by_sin[c] = ring.tile([P, GROUPS, width(c)], F32, name="by_sin", bufs=2)
            table = slice((t % 2) * DK, (t % 2 + 1) * DK)
            nc.vector.tensor_tensor(
                out=by_cos[c][:, t, :].rearrange("p (h d) -> p h d", d=DK),
                in0=acc[c, t].rearrange("p (h d) -> p h d", d=DK),
                in1=cos_sb[:, table].unsqueeze(1).to_broadcast([P, heads(c), DK]),
                op=ALU.mult,
            )
            nc.vector.tensor_tensor(
                out=by_sin[c][:, t, :].rearrange("p (h m e) -> p h m e", m=DK // 2, e=2),
                in0=acc[c, t].rearrange("p (h m e) -> p h m e", m=DK // 2, e=2)[:, :, :, ::-1],
                in1=sin_signed[:, table]
                .rearrange("p (m e) -> p m e", e=2)
                .unsqueeze(1)
                .to_broadcast([P, heads(c), DK // 2, 2]),
                op=ALU.mult,
            )

        def add(engine, c, half, h0, h1, rows=slice(0, 2)):
            if h0 == h1:
                return
            if (c, half) not in rotated:
                if half == 1 and c + 2 <= last:
                    rotated[c, half] = shared_tile(c + 2, [P, heads(c), 2, DK], F32)
                else:
                    rotated[c, half] = ring.tile([P, heads(c), 2, DK], F32, name="rotated", bufs=3)
            pair = slice(2 * half, 2 * half + 2)
            engine.tensor_tensor(
                out=rotated[c, half][:, h0:h1, rows, :],
                in0=by_cos[c][:, pair, :].rearrange("p j (h d) -> p h j d", d=DK)[:, h0:h1, rows, :],
                in1=by_sin[c][:, pair, :].rearrange("p j (h d) -> p h j d", d=DK)[:, h0:h1, rows, :],
                op=ALU.add,
            )

        def store(c, half, h0, h1):
            m, n0, cw = chunks[c]
            for r in range(2):
                nc.sync.dma_start(
                    out=outs[m][2 * half + r, n0 // DK + h0 : n0 // DK + h1].rearrange("h (q j) d -> q h (j d)", j=2),
                    in_=rotated[c, half][r:P:2, h0:h1].rearrange("p h j d -> p h (j d)"),
                )

        def gpsimd_heads(c):
            return heads(c) - V_HEADS if width(c) == N else 0

        for g in range(PASSES):
            load_w(0, 0, N, g)
            load_x(g)
        load_table(cos_sb, cos2)
        load_table(sin_sb, sin2)
        for n0 in range(N, E, N):
            for g in range(PASSES):
                load_w(0, n0, N, g)

        make_identity(nc, ident[:])
        nc.gpsimd.memset(signs[:], 1.0)
        nc.gpsimd.memset(signs[:, 0::2], -1.0)

        for g in range(PASSES):
            interleave(0, g, HEAD_V_COLS)
            if g > 0:
                quantize_x(g - 1)
            quantize_w(0, g)
            transpose_x(g)
            copy_x(g)
        nc.vector.tensor_tensor(out=sin_signed[:], in0=sin_sb[:], in1=signs[:], op=ALU.mult)
        interleave(1, 0, HEAD_V_COLS)
        quantize_x(GROUPS - 1)
        for t in range(GROUPS):
            multiply(0, t, range(PASSES))

        for c in range(last + 1):
            if c in (1, 3):
                for g in range(PASSES):
                    load_w(1, (c - 1) * N, 2 * N, g)
            if c > 0:
                quantize_w(c, 2)
                quantize_w(c, 3)
                add(nc.vector, c - 1, 0, gpsimd_heads(c - 1), heads(c - 1))
                store(c - 1, 0, 0, heads(c - 1))
                for t in range(GROUPS):
                    multiply(c, t, (2, 3))
            if c < last:
                if c > 0:
                    interleave(c + 1, 0, 0)
                interleave(c + 1, 1, HEAD_V_COLS if c == 0 else V_COLS if width(c + 1) == N else V_LAST)
                quantize_w(c + 1, 0)
                quantize_w(c + 1, 1)
                interleave(c + 1, 2, 0)
                interleave(c + 1, 3, 0)
            if c > 0:
                add(nc.gpsimd if c < last else nc.vector, c - 1, 1, 0, heads(c - 1))
                store(c - 1, 1, 0, heads(c - 1))
            for t in range(GROUPS):
                if c < last:
                    multiply(c + 1, t, (0, 1))
                products(c, t)
                if c < last and t == 1:
                    add(nc.gpsimd, c, 0, 0, gpsimd_heads(c))
                if c == last and t < 2:
                    add(nc.gpsimd, c, 0, 0, heads(c), slice(t, t + 1))
        store(last, 0, 0, heads(last))
        for h0 in range(0, heads(last), G_TAIL):
            add(nc.vector, last, 1, h0, h0 + G_TAIL)
            store(last, 1, h0, h0 + G_TAIL)
